import numpy as np
import ml_dtypes


def mxq(x, axis, fmt="e4m3"):
    dtype, down = {"e4m3": (ml_dtypes.float8_e4m3fn, 7), "e5m2": (ml_dtypes.float8_e5m2, 14)}[fmt]
    v = np.moveaxis(np.asarray(x, np.float32).astype(ml_dtypes.bfloat16).astype(np.float64), axis, -1)
    blocks = v.reshape(v.shape[:-1] + (-1, 32))
    amax = np.abs(blocks).max(-1, keepdims=True)
    byte = np.maximum(np.where(amax > 0, np.frexp(amax)[1] - 1 + 127, 0) - down, 1)
    scale = np.exp2(byte - 127.0)
    codes = (blocks / scale).astype(np.float32).astype(dtype).astype(np.float64)
    return np.moveaxis((codes * scale).reshape(v.shape), -1, axis)


WIDE = False


def mx_kscale(k):
    if not WIDE:
        return np.ones(k)
    levels = np.array([10, -10, 5, -5, 0])
    a = np.random.permutation(np.resize(levels, k // 512 * 4)).reshape(k // 512, 4)
    idx = np.arange(k)
    return np.exp2(a[idx // 512, idx % 128 // 32])


BF16 = ml_dtypes.bfloat16


def bf(x):
    return np.asarray(x, np.float32).astype(BF16)


def f64(x):
    return np.asarray(x).astype(np.float64)


B, L, N, RS, D, H, A, F = 4, 4, 128, 16, 512, 8, 64, 2048
S = L * (N + RS)
EPS = 1e-05


def rmsnorm(x, w):
    return x / np.sqrt(np.mean(x * x, -1, keepdims=True) + EPS) * w


def silu(v):
    return v / (1.0 + np.exp(-v))


def setup_inputs():
    s, t = mx_kscale(D), mx_kscale(D)
    return {'o_attn': bf(np.random.standard_normal((B, S, D)) * 0.14 * s),
            'xm': bf(np.random.standard_normal((B, S, D))),
            'attn_o_w': bf(np.random.standard_normal((D, D)) * 3.0 / np.sqrt(D) / s[:, None]),
            'ffn_norm_w': bf((1.0 + 0.1 * np.random.standard_normal(D)) * t),
            'ffn_up_w': bf(np.random.standard_normal((D, 2 * F)) / np.sqrt(D) / t[:, None])}


def reference(o_attn, xm, attn_o_w, ffn_norm_w, ffn_up_w):
    x2 = (mxq(f64(o_attn), 2, 'e4m3') @ mxq(f64(attn_o_w), 0, 'e4m3')) + f64(xm)
    xn2 = rmsnorm(x2, f64(ffn_norm_w))
    u1, u2 = np.split(mxq(xn2, 2, 'e4m3') @ mxq(f64(ffn_up_w), 0, 'e4m3'), 2, axis=-1)
    return x2, silu(u1) * u2

@@ -1,0 +1,228 @@
+from contextlib import ExitStack
+
+import concourse.mybir as mybir
+from concourse.masks import make_identity
+
+F32 = mybir.dt.float32
+BF16 = mybir.dt.bfloat16
+U32 = mybir.dt.uint32
+U8 = mybir.dt.uint8
+FP8X4 = mybir.dt.float8_e4m3fn_x4
+ACT = mybir.ActivationFunctionType
+ALU = mybir.AluOpType
+
+P = 128
+PACK = 4
+D = P * PACK
+TOKENS = 4 * 576
+TILES = TOKENS // P
+PAIR = 2
+PAIRS = TILES // PAIR
+F = 2048
+N_PASS = 512
+CHUNKS = F // N_PASS
+LOAD_COLS = 2 * N_PASS
+EPS = 1e-5
+
+FLOPS = 2 * TOKENS * D * (D + 2 * F)
+
+
+def tile_model_pb_kernel(tc, o_attn, xm, attn_o_w, ffn_norm_w, ffn_up_w, out_0, out_1):
+    nc = tc.nc
+
+    o_rows = o_attn.flatten_outer_dims().rearrange("(p j) d -> p j d", j=TILES)
+    xm_rows = xm.flatten_outer_dims().rearrange("(p j) d -> p j d", j=TILES)
+    x2_rows = out_0.flatten_outer_dims().rearrange("(p j) d -> p j d", j=TILES)
+    h_rows = out_1.flatten_outer_dims().rearrange("(p j) f -> p j f", j=TILES)
+
+    with ExitStack() as ctx:
+        loads = ctx.enter_context(tc.tile_pool(name="loads", bufs=1))
+        consts = ctx.enter_context(tc.tile_pool(name="consts", bufs=1))
+        weights = ctx.enter_context(tc.tile_pool(name="weights", bufs=1))
+        regroup = ctx.enter_context(tc.tile_pool(name="regroup", bufs=3))
+        stage = ctx.enter_context(tc.tile_pool(name="stage", bufs=3))
+        gated = ctx.enter_context(tc.tile_pool(name="gated", bufs=4))
+        results = ctx.enter_context(tc.tile_pool(name="results", bufs=3))
+        psum_t = ctx.enter_context(tc.psum_pool(name="psum_t", bufs=1))
+        psum_x = ctx.enter_context(tc.psum_pool(name="psum_x", bufs=2))
+        psum_u = ctx.enter_context(tc.psum_pool(name="psum_u", bufs=2))
+
+        o_sb = []
+        xm_sb = []
+        for i in range(PAIRS):
+            o_sb.append(loads.tile([P, PAIR, D], BF16, name="o_sb%d" % i))
+            xm_sb.append(loads.tile([P, PAIR, D], BF16, name="xm_sb%d" % i))
+        wo_raw = loads.tile([P, PACK, D], BF16)
+        up_raw = []
+        for b in range(2 * F // LOAD_COLS):
+            up_raw.append(loads.tile([P, PACK, LOAD_COLS], BF16, name="up_raw%d" % b))
+        gain_row = consts.tile([P, D], BF16)
+        nc.vector.memset(gain_row[:], 0.0)
+
+        def load_pair(i):
+            tiles = slice(PAIR * i, PAIR * (i + 1))
+            nc.sync.dma_start(out=o_sb[i][:], in_=o_rows[:, tiles, :])
+            nc.sync.dma_start(out=xm_sb[i][:], in_=xm_rows[:, tiles, :])
+
+        load_pair(0)
+        for u in range(2):
+            nc.sync.dma_start(
+                out=wo_raw[:, 2 * u : 2 * u + 2, :],
+                in_=attn_o_w[2 * P * u : 2 * P * (u + 1), :].rearrange("(p e) n -> p e n", e=2),
+            )
+        nc.sync.dma_start(out=gain_row[0:1, :], in_=ffn_norm_w.unsqueeze(0))
+        up_rows = ffn_up_w.rearrange("(t p) n -> p t n", p=P)
+        for b in range(len(up_raw)):
+            first = (b % 2) * F + (b // 2) * LOAD_COLS
+            nc.sync.dma_start(out=up_raw[b][:], in_=up_rows[:, :, first : first + LOAD_COLS])
+        for i in range(1, PAIRS):
+            load_pair(i)
+
+        ident_f32 = consts.tile([P, P], F32)
+        make_identity(nc, ident_f32[:])
+        ident_bf16 = consts.tile([P, P], BF16)
+        make_identity(nc, ident_bf16[:])
+        ones = consts.tile([P, P], BF16)
+        nc.vector.memset(ones[:], 1.0)
+        neg_half = consts.tile([P, PAIR], F32)
+        nc.vector.memset(neg_half[:], -0.5)
+
+        gain_ps = psum_x.tile([P, D], F32, tag="acc")
+        nc.tensor.matmul(out=gain_ps[:], lhsT=ones[:], rhs=gain_row[:], start=True, stop=True)
+        gain = consts.tile([P, D], F32)
+        nc.vector.tensor_copy(out=gain[:], in_=gain_ps[:])
+
+        def quantise_weight(copy_engine, raw_cols, name):
+            grouped = regroup.tile([P, N_PASS, PACK], BF16, tag="grouped", align_bytes=64)
+            copy_engine(
+                out=grouped[:].rearrange("p (c i) t -> p c t i", i=4),
+                in_=raw_cols.rearrange("p t (c i) -> p c t i", i=4),
+            )
+            codes = weights.tile([P, N_PASS], U32, name=name + "_codes", align_bytes=64)
+            scales = weights.tile([P, N_PASS], U8, name=name + "_scales", align_bytes=64)
+            nc.vector.quantize_mx(
+                out=codes[:].bitcast(FP8X4),
+                scales=scales[:],
+                in_=grouped[:].rearrange("p w t -> p (w t)"),
+            )
+            return codes, scales
+
+        wo_codes, wo_scales = quantise_weight(nc.vector.tensor_copy, wo_raw[:], "wo")
+
+        def project(i):
+            words = o_sb[i][:].bitcast(F32)
+            oT = psum_t.tile([P, PAIR, 2, P], F32)
+            for a in range(PAIR):
+                for u in range(2):
+                    nc.tensor.transpose(oT[:, a, u, :], words[:, a, P * u : P * (u + 1)], ident_f32[:])
+            o_grouped = stage.tile([P, PAIR * P * PACK], BF16, align_bytes=64)
+            nc.scalar.copy(
+                out=o_grouped[:].bitcast(F32).rearrange("p (a r u) -> p a r u", a=PAIR, u=2),
+                in_=oT[:].rearrange("p a u r -> p a r u"),
+            )
+            o_codes = stage.tile([P, PAIR * P], U32, align_bytes=64)
+            o_scales = stage.tile([P, PAIR * P], U8, align_bytes=64)
+            nc.vector.quantize_mx(out=o_codes[:].bitcast(FP8X4), scales=o_scales[:], in_=o_grouped[:])
+
+            x2 = stage.tile([P, PAIR, D], F32)
+            mean_sq = stage.tile([P, PAIR], F32)
+            for a in range(PAIR):
+                rows = slice(P * a, P * (a + 1))
+                acc = psum_x.tile([P, D], F32, tag="acc")
+                nc.tensor.matmul_mx(
+                    out=acc[:],
+                    lhsT=o_codes[:, rows].bitcast(FP8X4),
+                    lhsT_scale=o_scales[:, rows],
+                    rhs=wo_codes[:].bitcast(FP8X4),
+                    rhs_scale=wo_scales[:],
+                    start=True,
+                    stop=True,
+                )
+                nc.vector.tensor_tensor(out=x2[:, a, :], in0=acc[:], in1=xm_sb[i][:, a, :], op=ALU.add)
+                squares = stage.tile([P, D], BF16)
+                nc.scalar.activation(
+                    out=squares[:],
+                    in_=x2[:, a, :],
+                    func=ACT.Square,
+                    scale=D**-0.5,
+                    accum_out=mean_sq[:, a : a + 1],
+                )
+            nc.sync.dma_start(out=x2_rows[:, PAIR * i : PAIR * (i + 1), :], in_=x2[:])
+            shifted = stage.tile([P, PAIR], F32)
+            nc.gpsimd.tensor_scalar(
+                out=shifted[:], in0=mean_sq[:], scalar1=1.0, scalar2=EPS, op0=ALU.mult, op1=ALU.add
+            )
+            rstd = stage.tile([P, PAIR], F32)
+            nc.gpsimd.tensor_tensor(out=rstd[:], in0=shifted[:], in1=neg_half[:], op=ALU.pow)
+            return x2, rstd
+
+        def normalise(x2, rstd):
+            xn = stage.tile([P, PAIR, D], BF16)
+            for a in range(PAIR):
+                nc.vector.scalar_tensor_tensor(
+                    out=xn[:, a, :],
+                    in0=x2[:, a, :],
+                    scalar=rstd[:, a : a + 1],
+                    in1=gain[:],
+                    op0=ALU.mult,
+                    op1=ALU.mult,
+                )
+            xnT = psum_t.tile([P, PAIR, PACK, P], BF16)
+            for a in range(PAIR):
+                for t in range(PACK):
+                    nc.tensor.transpose(xnT[:, a, t, :], xn[:, a, P * t : P * (t + 1)], ident_bf16[:])
+            xn_grouped = stage.tile([P, PAIR, P, PACK], BF16, align_bytes=64)
+            nc.scalar.copy(out=xn_grouped[:], in_=xnT[:].rearrange("p a t r -> p a r t"))
+            xn_codes = stage.tile([P, PAIR * P], U32, align_bytes=64)
+            xn_scales = stage.tile([P, PAIR * P], U8, align_bytes=64)
+            nc.vector.quantize_mx(
+                out=xn_codes[:].bitcast(FP8X4),
+                scales=xn_scales[:],
+                in_=xn_grouped[:].rearrange("p a r t -> p (a r t)"),
+            )
+            return xn_codes, xn_scales
+
+        def gate(i, xn_codes, xn_scales):
+            for a in range(PAIR):
+                rows = slice(P * a, P * (a + 1))
+                h = results.tile([P, F], F32)
+                for c in range(CHUNKS):
+                    halves = []
+                    for half in range(2):
+                        codes, scales = up_q[half][c]
+                        u_ps = psum_u.tile([P, N_PASS], F32, name="u%d" % half)
+                        nc.tensor.matmul_mx(
+                            out=u_ps[:],
+                            lhsT=xn_codes[:, rows].bitcast(FP8X4),
+                            lhsT_scale=xn_scales[:, rows],
+                            rhs=codes[:].bitcast(FP8X4),
+                            rhs_scale=scales[:],
+                            start=True,
+                            stop=True,
+                        )
+                        halves.append(u_ps)
+                    silu = gated.tile([P, N_PASS], F32)
+                    nc.scalar.activation(out=silu[:], in_=halves[0][:], func=ACT.Silu)
+                    nc.vector.tensor_tensor(
+                        out=h[:, N_PASS * c : N_PASS * (c + 1)], in0=halves[1][:], in1=silu[:], op=ALU.mult
+                    )
+                nc.sync.dma_start(out=h_rows[:, PAIR * i + a, :], in_=h[:])
+
+        projected = {0: project(0)}
+
+        up_q = [[], []]
+        for c in range(CHUNKS):
+            for half in range(2):
+                raw = up_raw[2 * (c // 2) + half]
+                cols = slice(N_PASS * (c % 2), N_PASS * (c % 2 + 1))
+                engine_copy = nc.vector.tensor_copy if half == 0 else nc.scalar.copy
+                up_q[half].append(quantise_weight(engine_copy, raw[:, :, cols], "up%d_%d" % (half, c)))
+
+        projected[1] = project(1)
+        normed = {0: normalise(*projected[0])}
+        for i in range(PAIRS):
+            if i + 2 < PAIRS:
+                projected[i + 2] = project(i + 2)
+            if i + 1 < PAIRS:
+                normed[i + 1] = normalise(*projected[i + 1])
+            gate(i, *normed[i])

@@ -21,7 +21,7 @@ PAIRS = TILES // PAIR
 F = 2048
 N_PASS = 512
 CHUNKS = F // N_PASS
-LOAD_COLS = 2 * N_PASS
+LEAD = 6
 EPS = 1e-5
 
 FLOPS = 2 * TOKENS * D * (D + 2 * F)
@@ -36,46 +36,47 @@ def tile_model_pb_kernel(tc, o_attn, xm, attn_o_w, ffn_norm_w, ffn_up_w, out_0, 
     h_rows = out_1.flatten_outer_dims().rearrange("(p j) f -> p j f", j=TILES)
 
     with ExitStack() as ctx:
+        ctx.enter_context(tc.manual_schedule())
         loads = ctx.enter_context(tc.tile_pool(name="loads", bufs=1))
         consts = ctx.enter_context(tc.tile_pool(name="consts", bufs=1))
         weights = ctx.enter_context(tc.tile_pool(name="weights", bufs=1))
-        regroup = ctx.enter_context(tc.tile_pool(name="regroup", bufs=3))
-        stage = ctx.enter_context(tc.tile_pool(name="stage", bufs=3))
+        regroup = ctx.enter_context(tc.tile_pool(name="regroup", bufs=4))
+        stage = ctx.enter_context(tc.tile_pool(name="stage", bufs=4))
         gated = ctx.enter_context(tc.tile_pool(name="gated", bufs=4))
         results = ctx.enter_context(tc.tile_pool(name="results", bufs=3))
-        psum_t = ctx.enter_context(tc.psum_pool(name="psum_t", bufs=1))
-        psum_x = ctx.enter_context(tc.psum_pool(name="psum_x", bufs=2))
-        psum_u = ctx.enter_context(tc.psum_pool(name="psum_u", bufs=2))
+        psum = ctx.enter_context(tc.psum_pool(name="psum", bufs=1))
+
+        gain_row = consts.tile([P, D], BF16)
+        nc.vector.memset(gain_row[:], 0.0)
+        nc.sync.dma_start(out=gain_row[0:1, :], in_=ffn_norm_w.unsqueeze(0))
 
         o_sb = []
         xm_sb = []
-        for i in range(PAIRS):
-            o_sb.append(loads.tile([P, PAIR, D], BF16, name="o_sb%d" % i))
-            xm_sb.append(loads.tile([P, PAIR, D], BF16, name="xm_sb%d" % i))
-        wo_raw = loads.tile([P, PACK, D], BF16)
-        up_raw = []
-        for b in range(2 * F // LOAD_COLS):
-            up_raw.append(loads.tile([P, PACK, LOAD_COLS], BF16, name="up_raw%d" % b))
-        gain_row = consts.tile([P, D], BF16)
-        nc.vector.memset(gain_row[:], 0.0)
 
         def load_pair(i):
             tiles = slice(PAIR * i, PAIR * (i + 1))
+            o_sb.append(loads.tile([P, PAIR, D], BF16, name="o_sb%d" % i))
             nc.sync.dma_start(out=o_sb[i][:], in_=o_rows[:, tiles, :])
+            xm_sb.append(loads.tile([P, PAIR, D], BF16, name="xm_sb%d" % i))
             nc.sync.dma_start(out=xm_sb[i][:], in_=xm_rows[:, tiles, :])
 
         load_pair(0)
+        wo_raw = loads.tile([P, PACK, D], BF16)
         for u in range(2):
             nc.sync.dma_start(
                 out=wo_raw[:, 2 * u : 2 * u + 2, :],
                 in_=attn_o_w[2 * P * u : 2 * P * (u + 1), :].rearrange("(p e) n -> p e n", e=2),
             )
-        nc.sync.dma_start(out=gain_row[0:1, :], in_=ffn_norm_w.unsqueeze(0))
         up_rows = ffn_up_w.rearrange("(t p) n -> p t n", p=P)
-        for b in range(len(up_raw)):
-            first = (b % 2) * F + (b // 2) * LOAD_COLS
-            nc.sync.dma_start(out=up_raw[b][:], in_=up_rows[:, :, first : first + LOAD_COLS])
-        for i in range(1, PAIRS):
+        up_raw = [[], []]
+        for c in range(CHUNKS):
+            for half in range(2):
+                raw = loads.tile([P, PACK, N_PASS], BF16, name="up_raw%d_%d" % (half, c))
+                first = F * half + N_PASS * c
+                nc.sync.dma_start(out=raw[:], in_=up_rows[:, :, first : first + N_PASS])
+                up_raw[half].append(raw)
+            load_pair(c + 1)
+        for i in range(CHUNKS + 1, PAIRS):
             load_pair(i)
 
         ident_f32 = consts.tile([P, P], F32)
@@ -84,20 +85,23 @@ def tile_model_pb_kernel(tc, o_attn, xm, attn_o_w, ffn_norm_w, ffn_up_w, out_0, 
         make_identity(nc, ident_bf16[:])
         ones = consts.tile([P, P], BF16)
         nc.vector.memset(ones[:], 1.0)
-        neg_half = consts.tile([P, PAIR], F32)
+        neg_half = consts.tile([P, 1], F32)
         nc.vector.memset(neg_half[:], -0.5)
 
-        gain_ps = psum_x.tile([P, D], F32, tag="acc")
+        gain_ps = psum.tile([P, D], F32, tag="acc")
         nc.tensor.matmul(out=gain_ps[:], lhsT=ones[:], rhs=gain_row[:], start=True, stop=True)
         gain = consts.tile([P, D], F32)
         nc.vector.tensor_copy(out=gain[:], in_=gain_ps[:])
 
-        def quantise_weight(copy_engine, raw_cols, name):
+        def regroup_weight(copy_engine, raw):
             grouped = regroup.tile([P, N_PASS, PACK], BF16, tag="grouped", align_bytes=64)
             copy_engine(
                 out=grouped[:].rearrange("p (c i) t -> p c t i", i=4),
-                in_=raw_cols.rearrange("p t (c i) -> p c t i", i=4),
+                in_=raw[:].rearrange("p t (c i) -> p c t i", i=4),
             )
+            return grouped
+
+        def quantise_weight(grouped, name):
             codes = weights.tile([P, N_PASS], U32, name=name + "_codes", align_bytes=64)
             scales = weights.tile([P, N_PASS], U8, name=name + "_scales", align_bytes=64)
             nc.vector.quantize_mx(
@@ -107,122 +111,129 @@ def tile_model_pb_kernel(tc, o_attn, xm, attn_o_w, ffn_norm_w, ffn_up_w, out_0, 
             )
             return codes, scales
 
-        wo_codes, wo_scales = quantise_weight(nc.vector.tensor_copy, wo_raw[:], "wo")
+        wo_q = []
+        up_grouped = {}
+        up_q = {}
 
-        def project(i):
-            words = o_sb[i][:].bitcast(F32)
-            oT = psum_t.tile([P, PAIR, 2, P], F32)
-            for a in range(PAIR):
-                for u in range(2):
-                    nc.tensor.transpose(oT[:, a, u, :], words[:, a, P * u : P * (u + 1)], ident_f32[:])
-            o_grouped = stage.tile([P, PAIR * P * PACK], BF16, align_bytes=64)
-            nc.scalar.copy(
-                out=o_grouped[:].bitcast(F32).rearrange("p (a r u) -> p a r u", a=PAIR, u=2),
-                in_=oT[:].rearrange("p a u r -> p a r u"),
-            )
-            o_codes = stage.tile([P, PAIR * P], U32, align_bytes=64)
-            o_scales = stage.tile([P, PAIR * P], U8, align_bytes=64)
-            nc.vector.quantize_mx(out=o_codes[:].bitcast(FP8X4), scales=o_scales[:], in_=o_grouped[:])
+        def prepare_weights(it):
+            if it == -LEAD:
+                wo_q.extend(quantise_weight(regroup_weight(nc.vector.tensor_copy, wo_raw), "wo"))
+            c = it + LEAD - 1
+            if 0 <= c < CHUNKS:
+                up_grouped[0, c] = regroup_weight(nc.vector.tensor_copy, up_raw[0][c])
+                up_grouped[1, c] = regroup_weight(nc.scalar.copy, up_raw[1][c])
+            if 0 <= c - 1 < CHUNKS:
+                for half in range(2):
+                    up_q[half, c - 1] = quantise_weight(up_grouped[half, c - 1], "up%d_%d" % (half, c - 1))
 
-            x2 = stage.tile([P, PAIR, D], F32)
-            mean_sq = stage.tile([P, PAIR], F32)
-            for a in range(PAIR):
-                rows = slice(P * a, P * (a + 1))
-                acc = psum_x.tile([P, D], F32, tag="acc")
+        live = {}
+
+        def in_range(j):
+            return 0 <= j < TILES
+
+        def first_stage(it):
+            ja, jb, jc, jd, je = it + 6, it + 5, it + 4, it + 3, it + 2
+            if in_range(jb):
+                acc = psum.tile([P, D], F32, tag="acc")
                 nc.tensor.matmul_mx(
                     out=acc[:],
-                    lhsT=o_codes[:, rows].bitcast(FP8X4),
-                    lhsT_scale=o_scales[:, rows],
-                    rhs=wo_codes[:].bitcast(FP8X4),
-                    rhs_scale=wo_scales[:],
+                    lhsT=live["o_codes", jb][:].bitcast(FP8X4),
+                    lhsT_scale=live["o_scales", jb][:],
+                    rhs=wo_q[0][:].bitcast(FP8X4),
+                    rhs_scale=wo_q[1][:],
                     start=True,
                     stop=True,
                 )
-                nc.vector.tensor_tensor(out=x2[:, a, :], in0=acc[:], in1=xm_sb[i][:, a, :], op=ALU.add)
-                squares = stage.tile([P, D], BF16)
-                nc.scalar.activation(
-                    out=squares[:],
-                    in_=x2[:, a, :],
-                    func=ACT.Square,
-                    scale=D**-0.5,
-                    accum_out=mean_sq[:, a : a + 1],
-                )
-            nc.sync.dma_start(out=x2_rows[:, PAIR * i : PAIR * (i + 1), :], in_=x2[:])
-            shifted = stage.tile([P, PAIR], F32)
-            nc.gpsimd.tensor_scalar(
-                out=shifted[:], in0=mean_sq[:], scalar1=1.0, scalar2=EPS, op0=ALU.mult, op1=ALU.add
-            )
-            rstd = stage.tile([P, PAIR], F32)
-            nc.gpsimd.tensor_tensor(out=rstd[:], in0=shifted[:], in1=neg_half[:], op=ALU.pow)
-            return x2, rstd
+            if in_range(ja):
+                words = o_sb[ja // PAIR][:].bitcast(F32)
+                oT = psum.tile([P, 2, P], F32)
+                for u in range(2):
+                    nc.tensor.transpose(oT[:, u, :], words[:, ja % PAIR, P * u : P * (u + 1)], ident_f32[:])
+            if in_range(je):
+                xnT = psum.tile([P, PACK, P], BF16)
+                for t in range(PACK):
+                    nc.tensor.transpose(xnT[:, t, :], live["xn", je][:, P * t : P * (t + 1)], ident_bf16[:])
 
-        def normalise(x2, rstd):
-            xn = stage.tile([P, PAIR, D], BF16)
-            for a in range(PAIR):
+            if in_range(jb):
+                x2 = stage.tile([P, D], F32)
+                live["x2", jb] = x2
+                nc.vector.tensor_tensor(out=x2[:], in0=acc[:], in1=xm_sb[jb // PAIR][:, jb % PAIR, :], op=ALU.add)
+                nc.sync.dma_start(out=x2_rows[:, jb, :], in_=x2[:])
+            if in_range(jc):
+                squares = stage.tile([P, D], BF16)
+                mean_sq = stage.tile([P, 1], F32)
+                nc.scalar.activation(
+                    out=squares[:], in_=live["x2", jc][:], func=ACT.Square, scale=D**-0.5, accum_out=mean_sq[:]
+                )
+                shifted = stage.tile([P, 1], F32)
+                nc.gpsimd.tensor_scalar(
+                    out=shifted[:], in0=mean_sq[:], scalar1=1.0, scalar2=EPS, op0=ALU.mult, op1=ALU.add
+                )
+                rstd = stage.tile([P, 1], F32)
+                live["rstd", jc] = rstd
+                nc.gpsimd.tensor_tensor(out=rstd[:], in0=shifted[:], in1=neg_half[:], op=ALU.pow)
+            if in_range(jd):
+                xn = stage.tile([P, D], BF16)
+                live["xn", jd] = xn
                 nc.vector.scalar_tensor_tensor(
-                    out=xn[:, a, :],
-                    in0=x2[:, a, :],
-                    scalar=rstd[:, a : a + 1],
+                    out=xn[:],
+                    in0=live["x2", jd][:],
+                    scalar=live["rstd", jd][:],
                     in1=gain[:],
                     op0=ALU.mult,
                     op1=ALU.mult,
                 )
-            xnT = psum_t.tile([P, PAIR, PACK, P], BF16)
-            for a in range(PAIR):
-                for t in range(PACK):
-                    nc.tensor.transpose(xnT[:, a, t, :], xn[:, a, P * t : P * (t + 1)], ident_bf16[:])
-            xn_grouped = stage.tile([P, PAIR, P, PACK], BF16, align_bytes=64)
-            nc.scalar.copy(out=xn_grouped[:], in_=xnT[:].rearrange("p a t r -> p a r t"))
-            xn_codes = stage.tile([P, PAIR * P], U32, align_bytes=64)
-            xn_scales = stage.tile([P, PAIR * P], U8, align_bytes=64)
-            nc.vector.quantize_mx(
-                out=xn_codes[:].bitcast(FP8X4),
-                scales=xn_scales[:],
-                in_=xn_grouped[:].rearrange("p a r t -> p (a r t)"),
-            )
-            return xn_codes, xn_scales
+            if in_range(ja):
+                o_grouped = stage.tile([P, P * PACK], BF16, align_bytes=64)
+                nc.scalar.copy(
+                    out=o_grouped[:].bitcast(F32).rearrange("p (r u) -> p r u", u=2),
+                    in_=oT[:].rearrange("p u r -> p r u"),
+                )
+                o_codes = stage.tile([P, P], U32, align_bytes=64)
+                o_scales = stage.tile([P, P], U8, align_bytes=64)
+                live["o_codes", ja] = o_codes
+                live["o_scales", ja] = o_scales
+                nc.vector.quantize_mx(out=o_codes[:].bitcast(FP8X4), scales=o_scales[:], in_=o_grouped[:])
+            if in_range(je):
+                xn_grouped = stage.tile([P, P, PACK], BF16, align_bytes=64)
+                nc.scalar.copy(out=xn_grouped[:], in_=xnT[:].rearrange("p t r -> p r t"))
+                xn_codes = stage.tile([P, P], U32, align_bytes=64)
+                xn_scales = stage.tile([P, P], U8, align_bytes=64)
+                live["xn_codes", je] = xn_codes
+                live["xn_scales", je] = xn_scales
+                nc.vector.quantize_mx(
+                    out=xn_codes[:].bitcast(FP8X4),
+                    scales=xn_scales[:],
+                    in_=xn_grouped[:].rearrange("p r t -> p (r t)"),
+                )
 
-        def gate(i, xn_codes, xn_scales):
-            for a in range(PAIR):
-                rows = slice(P * a, P * (a + 1))
-                h = results.tile([P, F], F32)
-                for c in range(CHUNKS):
-                    halves = []
-                    for half in range(2):
-                        codes, scales = up_q[half][c]
-                        u_ps = psum_u.tile([P, N_PASS], F32, name="u%d" % half)
-                        nc.tensor.matmul_mx(
-                            out=u_ps[:],
-                            lhsT=xn_codes[:, rows].bitcast(FP8X4),
-                            lhsT_scale=xn_scales[:, rows],
-                            rhs=codes[:].bitcast(FP8X4),
-                            rhs_scale=scales[:],
-                            start=True,
-                            stop=True,
-                        )
-                        halves.append(u_ps)
-                    silu = gated.tile([P, N_PASS], F32)
-                    nc.scalar.activation(out=silu[:], in_=halves[0][:], func=ACT.Silu)
-                    nc.vector.tensor_tensor(
-                        out=h[:, N_PASS * c : N_PASS * (c + 1)], in0=halves[1][:], in1=silu[:], op=ALU.mult
+        def second_stage(j):
+            h = results.tile([P, F], F32)
+            for c in range(CHUNKS):
+                halves = []
+                for half in range(2):
+                    codes, scales = up_q[half, c]
+                    u_ps = psum.tile([P, N_PASS], F32, name="u%d" % half, bufs=2 + half)
+                    nc.tensor.matmul_mx(
+                        out=u_ps[:],
+                        lhsT=live["xn_codes", j][:].bitcast(FP8X4),
+                        lhsT_scale=live["xn_scales", j][:],
+                        rhs=codes[:].bitcast(FP8X4),
+                        rhs_scale=scales[:],
+                        start=True,
+                        stop=True,
                     )
-                nc.sync.dma_start(out=h_rows[:, PAIR * i + a, :], in_=h[:])
+                    halves.append(u_ps)
+                silu = gated.tile([P, N_PASS], F32)
+                nc.scalar.activation(out=silu[:], in_=halves[0][:], func=ACT.Silu)
+                nc.vector.tensor_tensor(
+                    out=h[:, N_PASS * c : N_PASS * (c + 1)], in0=halves[1][:], in1=silu[:], op=ALU.mult
+                )
+            nc.sync.dma_start(out=h_rows[:, j, :], in_=h[:])
 
-        projected = {0: project(0)}
-
-        up_q = [[], []]
-        for c in range(CHUNKS):
-            for half in range(2):
-                raw = up_raw[2 * (c // 2) + half]
-                cols = slice(N_PASS * (c % 2), N_PASS * (c % 2 + 1))
-                engine_copy = nc.vector.tensor_copy if half == 0 else nc.scalar.copy
-                up_q[half].append(quantise_weight(engine_copy, raw[:, :, cols], "up%d_%d" % (half, c)))
-
-        projected[1] = project(1)
-        normed = {0: normalise(*projected[0])}
-        for i in range(PAIRS):
-            if i + 2 < PAIRS:
-                projected[i + 2] = project(i + 2)
-            if i + 1 < PAIRS:
-                normed[i + 1] = normalise(*projected[i + 1])
-            gate(i, *normed[i])
+        for it in range(-LEAD, TILES):
+            if it < 0:
+                prepare_weights(it)
+            else:
+                second_stage(it)
+            first_stage(it)

@@ -132,7 +132,7 @@ def tile_model_pb_kernel(tc, o_attn, xm, attn_o_w, ffn_norm_w, ffn_up_w, out_0, 
             return 0 <= j < TILES
 
         def first_stage(it):
-            ja, jb, jc, jd, je = it + 6, it + 5, it + 4, it + 3, it + 2
+            ja, jb, jc, je = it + 6, it + 5, it + 4, it + 2
             if in_range(jb):
                 acc = psum.tile([P, D], F32, tag="acc")
                 nc.tensor.matmul_mx(
@@ -154,6 +154,12 @@ def tile_model_pb_kernel(tc, o_attn, xm, attn_o_w, ffn_norm_w, ffn_up_w, out_0, 
                 for t in range(PACK):
                     nc.tensor.transpose(xnT[:, t, :], live["xn", je][:, P * t : P * (t + 1)], ident_bf16[:])
 
+            if in_range(ja):
+                o_grouped = stage.tile([P, P * PACK], BF16, align_bytes=64)
+                nc.vector.tensor_copy(
+                    out=o_grouped[:].bitcast(F32).rearrange("p (r u) -> p r u", u=2),
+                    in_=oT[:].rearrange("p u r -> p r u"),
+                )
             if in_range(jb):
                 x2 = stage.tile([P, D], F32)
                 live["x2", jb] = x2
@@ -170,25 +176,17 @@ def tile_model_pb_kernel(tc, o_attn, xm, attn_o_w, ffn_norm_w, ffn_up_w, out_0, 
                     out=shifted[:], in0=mean_sq[:], scalar1=1.0, scalar2=EPS, op0=ALU.mult, op1=ALU.add
                 )
                 rstd = stage.tile([P, 1], F32)
-                live["rstd", jc] = rstd
                 nc.gpsimd.tensor_tensor(out=rstd[:], in0=shifted[:], in1=neg_half[:], op=ALU.pow)
-            if in_range(jd):
                 xn = stage.tile([P, D], BF16)
-                live["xn", jd] = xn
-                nc.vector.scalar_tensor_tensor(
-                    out=xn[:],
-                    in0=live["x2", jd][:],
-                    scalar=live["rstd", jd][:],
-                    in1=gain[:],
-                    op0=ALU.mult,
-                    op1=ALU.mult,
+                live["xn", jc] = xn
+                nc.gpsimd.tensor_scalar(
+                    out=xn[:], in0=live["x2_gain", jc][:], scalar1=rstd[:], scalar2=1.0, op0=ALU.mult, op1=ALU.mult
                 )
+            if in_range(jb):
+                x2_gain = stage.tile([P, D], F32)
+                live["x2_gain", jb] = x2_gain
+                nc.gpsimd.tensor_tensor(out=x2_gain[:], in0=x2[:], in1=gain[:], op=ALU.mult)
             if in_range(ja):
-                o_grouped = stage.tile([P, P * PACK], BF16, align_bytes=64)
-                nc.scalar.copy(
-                    out=o_grouped[:].bitcast(F32).rearrange("p (r u) -> p r u", u=2),
-                    in_=oT[:].rearrange("p u r -> p r u"),
-                )
                 o_codes = stage.tile([P, P], U32, align_bytes=64)
                 o_scales = stage.tile([P, P], U8, align_bytes=64)
                 live["o_codes", ja] = o_codes

from contextlib import ExitStack

import concourse.mybir as mybir
from concourse.masks import make_identity

F32 = mybir.dt.float32
BF16 = mybir.dt.bfloat16
U32 = mybir.dt.uint32
U8 = mybir.dt.uint8
FP8X4 = mybir.dt.float8_e4m3fn_x4
ACT = mybir.ActivationFunctionType
ALU = mybir.AluOpType

P = 128
PACK = 4
D = P * PACK
TOKENS = 4 * 576
TILES = TOKENS // P
PAIR = 2
PAIRS = TILES // PAIR
F = 2048
N_PASS = 512
CHUNKS = F // N_PASS
LEAD = 6
EPS = 1e-5

FLOPS = 2 * TOKENS * D * (D + 2 * F)


def tile_model_pb_kernel(tc, o_attn, xm, attn_o_w, ffn_norm_w, ffn_up_w, out_0, out_1):
    nc = tc.nc

    o_rows = o_attn.flatten_outer_dims().rearrange("(p j) d -> p j d", j=TILES)
    xm_rows = xm.flatten_outer_dims().rearrange("(p j) d -> p j d", j=TILES)
    x2_rows = out_0.flatten_outer_dims().rearrange("(p j) d -> p j d", j=TILES)
    h_rows = out_1.flatten_outer_dims().rearrange("(p j) f -> p j f", j=TILES)

    with ExitStack() as ctx:
        ctx.enter_context(tc.manual_schedule())
        loads = ctx.enter_context(tc.tile_pool(name="loads", bufs=1))
        consts = ctx.enter_context(tc.tile_pool(name="consts", bufs=1))
        weights = ctx.enter_context(tc.tile_pool(name="weights", bufs=1))
        regroup = ctx.enter_context(tc.tile_pool(name="regroup", bufs=4))
        stage = ctx.enter_context(tc.tile_pool(name="stage", bufs=4))
        gated = ctx.enter_context(tc.tile_pool(name="gated", bufs=4))
        results = ctx.enter_context(tc.tile_pool(name="results", bufs=3))
        psum = ctx.enter_context(tc.psum_pool(name="psum", bufs=1))

        gain_row = consts.tile([P, D], BF16)
        nc.vector.memset(gain_row[:], 0.0)
        nc.sync.dma_start(out=gain_row[0:1, :], in_=ffn_norm_w.unsqueeze(0))

        o_sb = []
        xm_sb = []

        def load_pair(i):
            tiles = slice(PAIR * i, PAIR * (i + 1))
            o_sb.append(loads.tile([P, PAIR, D], BF16, name="o_sb%d" % i))
            nc.sync.dma_start(out=o_sb[i][:], in_=o_rows[:, tiles, :])
            xm_sb.append(loads.tile([P, PAIR, D], BF16, name="xm_sb%d" % i))
            nc.sync.dma_start(out=xm_sb[i][:], in_=xm_rows[:, tiles, :])

        load_pair(0)
        wo_raw = loads.tile([P, PACK, D], BF16)
        for u in range(2):
            nc.sync.dma_start(
                out=wo_raw[:, 2 * u : 2 * u + 2, :],
                in_=attn_o_w[2 * P * u : 2 * P * (u + 1), :].rearrange("(p e) n -> p e n", e=2),
            )
        up_rows = ffn_up_w.rearrange("(t p) n -> p t n", p=P)
        up_raw = [[], []]
        for c in range(CHUNKS):
            for half in range(2):
                raw = loads.tile([P, PACK, N_PASS], BF16, name="up_raw%d_%d" % (half, c))
                first = F * half + N_PASS * c
                nc.sync.dma_start(out=raw[:], in_=up_rows[:, :, first : first + N_PASS])
                up_raw[half].append(raw)
            load_pair(c + 1)
        for i in range(CHUNKS + 1, PAIRS):
            load_pair(i)

        ident_f32 = consts.tile([P, P], F32)
        make_identity(nc, ident_f32[:])
        ident_bf16 = consts.tile([P, P], BF16)
        make_identity(nc, ident_bf16[:])
        ones = consts.tile([P, P], BF16)
        nc.vector.memset(ones[:], 1.0)
        neg_half = consts.tile([P, 1], F32)
        nc.vector.memset(neg_half[:], -0.5)

        gain_ps = psum.tile([P, D], F32, tag="acc")
        nc.tensor.matmul(out=gain_ps[:], lhsT=ones[:], rhs=gain_row[:], start=True, stop=True)
        gain = consts.tile([P, D], F32)
        nc.vector.tensor_copy(out=gain[:], in_=gain_ps[:])

        def regroup_weight(copy_engine, raw):
            grouped = regroup.tile([P, N_PASS, PACK], BF16, tag="grouped", align_bytes=64)
            copy_engine(
                out=grouped[:].rearrange("p (c i) t -> p c t i", i=4),
                in_=raw[:].rearrange("p t (c i) -> p c t i", i=4),
            )
            return grouped

        def quantise_weight(grouped, name):
            codes = weights.tile([P, N_PASS], U32, name=name + "_codes", align_bytes=64)
            scales = weights.tile([P, N_PASS], U8, name=name + "_scales", align_bytes=64)
            nc.vector.quantize_mx(
                out=codes[:].bitcast(FP8X4),
                scales=scales[:],
                in_=grouped[:].rearrange("p w t -> p (w t)"),
            )
            return codes, scales

        wo_q = []
        up_grouped = {}
        up_q = {}

        def prepare_weights(it):
            if it == -LEAD:
                wo_q.extend(quantise_weight(regroup_weight(nc.vector.tensor_copy, wo_raw), "wo"))
            c = it + LEAD - 1
            if 0 <= c < CHUNKS:
                up_grouped[0, c] = regroup_weight(nc.vector.tensor_copy, up_raw[0][c])
                up_grouped[1, c] = regroup_weight(nc.scalar.copy, up_raw[1][c])
            if 0 <= c - 1 < CHUNKS:
                for half in range(2):
                    up_q[half, c - 1] = quantise_weight(up_grouped[half, c - 1], "up%d_%d" % (half, c - 1))

        live = {}

        def in_range(j):
            return 0 <= j < TILES

        def first_stage(it):
            ja, jb, jc, je = it + 6, it + 5, it + 4, it + 2
            if in_range(jb):
                acc = psum.tile([P, D], F32, tag="acc")
                nc.tensor.matmul_mx(
                    out=acc[:],
                    lhsT=live["o_codes", jb][:].bitcast(FP8X4),
                    lhsT_scale=live["o_scales", jb][:],
                    rhs=wo_q[0][:].bitcast(FP8X4),
                    rhs_scale=wo_q[1][:],
                    start=True,
                    stop=True,
                )
            if in_range(ja):
                words = o_sb[ja // PAIR][:].bitcast(F32)
                oT = psum.tile([P, 2, P], F32)
                for u in range(2):
                    nc.tensor.transpose(oT[:, u, :], words[:, ja % PAIR, P * u : P * (u + 1)], ident_f32[:])
            if in_range(je):
                xnT = psum.tile([P, PACK, P], BF16)
                for t in range(PACK):
                    nc.tensor.transpose(xnT[:, t, :], live["xn", je][:, P * t : P * (t + 1)], ident_bf16[:])

            if in_range(ja):
                o_grouped = stage.tile([P, P * PACK], BF16, align_bytes=64)
                nc.vector.tensor_copy(
                    out=o_grouped[:].bitcast(F32).rearrange("p (r u) -> p r u", u=2),
                    in_=oT[:].rearrange("p u r -> p r u"),
                )
            if in_range(jb):
                x2 = stage.tile([P, D], F32)
                live["x2", jb] = x2
                nc.vector.tensor_tensor(out=x2[:], in0=acc[:], in1=xm_sb[jb // PAIR][:, jb % PAIR, :], op=ALU.add)
                nc.sync.dma_start(out=x2_rows[:, jb, :], in_=x2[:])
            if in_range(jc):
                squares = stage.tile([P, D], BF16)
                mean_sq = stage.tile([P, 1], F32)
                nc.scalar.activation(
                    out=squares[:], in_=live["x2", jc][:], func=ACT.Square, scale=D**-0.5, accum_out=mean_sq[:]
                )
                shifted = stage.tile([P, 1], F32)
                nc.gpsimd.tensor_scalar(
                    out=shifted[:], in0=mean_sq[:], scalar1=1.0, scalar2=EPS, op0=ALU.mult, op1=ALU.add
                )
                rstd = stage.tile([P, 1], F32)
                nc.gpsimd.tensor_tensor(out=rstd[:], in0=shifted[:], in1=neg_half[:], op=ALU.pow)
                xn = stage.tile([P, D], BF16)
                live["xn", jc] = xn
                nc.gpsimd.tensor_scalar(
                    out=xn[:], in0=live["x2_gain", jc][:], scalar1=rstd[:], scalar2=1.0, op0=ALU.mult, op1=ALU.mult
                )
            if in_range(jb):
                x2_gain = stage.tile([P, D], F32)
                live["x2_gain", jb] = x2_gain
                nc.gpsimd.tensor_tensor(out=x2_gain[:], in0=x2[:], in1=gain[:], op=ALU.mult)
            if in_range(ja):
                o_codes = stage.tile([P, P], U32, align_bytes=64)
                o_scales = stage.tile([P, P], U8, align_bytes=64)
                live["o_codes", ja] = o_codes
                live["o_scales", ja] = o_scales
                nc.vector.quantize_mx(out=o_codes[:].bitcast(FP8X4), scales=o_scales[:], in_=o_grouped[:])
            if in_range(je):
                xn_grouped = stage.tile([P, P, PACK], BF16, align_bytes=64)
                nc.scalar.copy(out=xn_grouped[:], in_=xnT[:].rearrange("p t r -> p r t"))
                xn_codes = stage.tile([P, P], U32, align_bytes=64)
                xn_scales = stage.tile([P, P], U8, align_bytes=64)
                live["xn_codes", je] = xn_codes
                live["xn_scales", je] = xn_scales
                nc.vector.quantize_mx(
                    out=xn_codes[:].bitcast(FP8X4),
                    scales=xn_scales[:],
                    in_=xn_grouped[:].rearrange("p r t -> p (r t)"),
                )

        def second_stage(j):
            h = results.tile([P, F], F32)
            for c in range(CHUNKS):
                halves = []
                for half in range(2):
                    codes, scales = up_q[half, c]
                    u_ps = psum.tile([P, N_PASS], F32, name="u%d" % half, bufs=2 + half)
                    nc.tensor.matmul_mx(
                        out=u_ps[:],
                        lhsT=live["xn_codes", j][:].bitcast(FP8X4),
                        lhsT_scale=live["xn_scales", j][:],
                        rhs=codes[:].bitcast(FP8X4),
                        rhs_scale=scales[:],
                        start=True,
                        stop=True,
                    )
                    halves.append(u_ps)
                silu = gated.tile([P, N_PASS], F32)
                nc.scalar.activation(out=silu[:], in_=halves[0][:], func=ACT.Silu)
                nc.vector.tensor_tensor(
                    out=h[:, N_PASS * c : N_PASS * (c + 1)], in0=halves[1][:], in1=silu[:], op=ALU.mult
                )
            nc.sync.dma_start(out=h_rows[:, j, :], in_=h[:])

        for it in range(-LEAD, TILES):
            if it < 0:
                prepare_weights(it)
            else:
                second_stage(it)
            first_stage(it)
